import numpy as np
import ml_dtypes


def mxq(x, axis, fmt="e4m3"):
    dtype, down = {"e4m3": (ml_dtypes.float8_e4m3fn, 7), "e5m2": (ml_dtypes.float8_e5m2, 14)}[fmt]
    v = np.moveaxis(np.asarray(x, np.float32).astype(ml_dtypes.bfloat16).astype(np.float64), axis, -1)
    blocks = v.reshape(v.shape[:-1] + (-1, 32))
    amax = np.abs(blocks).max(-1, keepdims=True)
    byte = np.maximum(np.where(amax > 0, np.frexp(amax)[1] - 1 + 127, 0) - down, 1)
    scale = np.exp2(byte - 127.0)
    codes = (blocks / scale).astype(np.float32).astype(dtype).astype(np.float64)
    return np.moveaxis((codes * scale).reshape(v.shape), -1, axis)


WIDE = False


def mx_kscale(k):
    if not WIDE:
        return np.ones(k)
    levels = np.array([10, -10, 5, -5, 0])
    if k % 512:
        return np.exp2(np.random.permutation(np.resize(levels, k // 32))).repeat(32)
    a = np.empty((k // 512, 16))
    for p in range(k // 512):
        a[p, :8] = np.random.permutation(np.resize(levels, 8))
        for g in range(8):
            far = levels[np.abs(levels - a[p, g]) >= 10]
            a[p, g + 8] = far[np.random.randint(len(far))]
    return np.exp2(a.ravel()).repeat(32)


BF16 = ml_dtypes.bfloat16


def bf(x):
    return np.asarray(x, np.float32).astype(BF16)


def f64(x):
    return np.asarray(x).astype(np.float64)


B, T, C, R, H, DN, DR, DV = 2, 1024, 8192, 2048, 16, 128, 64, 128
DQ = DN + DR
NF = DR // 2


def rotate_half(u):
    u1, u2 = u[..., : u.shape[-1] // 2], u[..., u.shape[-1] // 2 :]
    return np.concatenate([-u2, u1], axis=-1)


def setup_inputs():
    s, t = mx_kscale(C), mx_kscale(R)
    return {
        "x": bf(np.random.standard_normal((B, T, C)) * s),
        "freqs_cis": bf(np.stack([np.random.uniform(size=(T, NF)), np.random.uniform(size=(T, NF))], axis=-1)),
        "w_kv_down": bf(np.random.standard_normal((C, R)) / np.sqrt(C) / s[:, None] * t),
        "w_k_up": bf(np.random.standard_normal((R, H * DQ)) / np.sqrt(R) / t[:, None]),
        "w_v_up": bf(np.random.standard_normal((R, H * DV)) / np.sqrt(R) / t[:, None]),
    }


def reference(x, freqs_cis, w_kv_down, w_k_up, w_v_up):
    kv = mxq(f64(x), 2, "e4m3") @ mxq(f64(w_kv_down), 0, "e4m3")
    kvq = mxq(kv, 2, "e4m3")
    k = (kvq @ mxq(f64(w_k_up), 0, "e4m3")).reshape(B, T, H, DQ)
    v = (kvq @ mxq(f64(w_v_up), 0, "e4m3")).reshape(B, T, H, DV)
    k_nope, k_rope = k[..., :DN], k[..., DN:]
    freqs = f64(freqs_cis)
    cos = freqs[..., 0][None, :, None, :]
    sin = freqs[..., 1][None, :, None, :]
    rep = DR // cos.shape[-1]
    cos = np.tile(cos, (1, 1, 1, rep))
    sin = np.tile(sin, (1, 1, 1, rep))
    k_rope = k_rope * cos + rotate_half(k_rope) * sin
    return np.concatenate([k_nope, k_rope], axis=-1), v

@@ -1,0 +1,327 @@
+from contextlib import ExitStack
+
+import concourse.mybir as mybir
+from concourse.masks import make_identity
+
+FLOPS = 2 * 2048 * 8192 * 2048 + 2 * 2048 * 2048 * 5120
+
+F32 = mybir.dt.float32
+BF16 = mybir.dt.bfloat16
+U32 = mybir.dt.uint32
+U8 = mybir.dt.uint8
+FP8X4 = mybir.dt.float8_e4m3fn_x4
+
+P = 128
+NG = 16
+NQ = 4
+NB = 17
+LD = 3
+GROUPS = (("k", 0), ("v", 0), ("k", 1), ("v", 1))
+CELL_BANKS = (4, 5, 6, 7, 0, 1, 2, 3)
+HALF_CHUNKS = ((0, 0), (0, 1), (0, 2), (0, 3), (1, 0), (1, 1), (1, 2))
+SRT_TAGS = ("kc0_2", "kc0_3", "kc1_2", "kc1_3", "kc2_2", "kc2_3")
+
+
+def tile_fa3mlaattention_pa_l_kernel(tc, x, freqs_cis, w_kv_down, w_k_up, w_v_up, out_0, out_1):
+    nc = tc.nc
+    with ExitStack() as ctx:
+        sb = ctx.enter_context(tc.tile_pool(name="sb", bufs=1))
+        ps = ctx.enter_context(tc.psum_pool(name="ps", bufs=1))
+        ctx.enter_context(tc.manual_schedule())
+
+        x_units = x.rearrange("b (n a p) k -> b n p a k", a=4, p=P)
+        wd = w_kv_down.rearrange("(g p j) c -> g p j c", p=P, j=4)
+        wk = w_k_up.rearrange("(q p j) c -> q p j c", p=P, j=4)
+        wv = w_v_up.rearrange("(q p j) c -> q p j c", p=P, j=4)
+        k_out = out_0.rearrange("b (a p) h d -> b a p (h d)", p=P)
+        v_out = out_1.rearrange("b (a p) h d -> b a p (h d)", p=P)
+
+        ident = sb.tile([P, P], F32, name="ident")
+        make_identity(nc, ident[:])
+        fr = sb.tile([P, 8, 64], BF16, name="fr")
+
+        pieces = []
+        w_piece = {}
+        for h, c in HALF_CHUNKS:
+            for g in range(NG):
+                w_piece[(h, c, g)] = len(pieces)
+                pieces.append((wd[g, :, :, 512 * c : 512 * (c + 1)], True))
+        for g in range(NG):
+            w_piece[(1, 3, g)] = w_piece[(0, 3, g)]
+        group_piece = {}
+        for kind, grp_i in GROUPS:
+            width = 3 if kind == "k" else 2
+            src = wk if kind == "k" else wv
+            for jj in range(width):
+                col = 512 * (width * grp_i + jj)
+                for q in range(NQ):
+                    group_piece[(kind, grp_i, jj, q)] = len(pieces)
+                    pieces.append((src[q, :, :, col : col + 512], False))
+        n_pieces = len(pieces)
+        n_w = len(HALF_CHUNKS) * NG
+
+        raws = {}
+        grouped = {}
+        codes = {}
+        st = {"q": 0, "avail": NB, "bank": 4}
+
+        def load(s):
+            raw = sb.tile([P, 4, 512], BF16, tag="raw", bufs=LD + 1, name="raw")
+            nc.sync.dma_start(out=raw[:], in_=pieces[s][0])
+            raws[s] = raw
+
+        def interleave(grp, raw, permuted, mv):
+            if permuted:
+                dst = grp[:].rearrange("p (t m j) -> p t m j", t=4, j=4)
+                src = raw[:].rearrange("p j (m t) -> p t m j", t=4)
+                nc.vector.tensor_copy(out=dst[:, :, 0:mv, :], in_=src[:, :, 0:mv, :])
+                nc.scalar.copy(out=dst[:, :, mv:P, :], in_=src[:, :, mv:P, :])
+            else:
+                dst = grp[:].rearrange("p (c j) -> p c j", j=4)
+                src = raw[:].rearrange("p j c -> p c j")
+                nc.vector.tensor_copy(out=dst[:, 0 : 4 * mv, :], in_=src[:, 0 : 4 * mv, :])
+                nc.scalar.copy(out=dst[:, 4 * mv : 512, :], in_=src[:, 4 * mv : 512, :])
+
+        def copy(s, mv):
+            grp = sb.tile([P, 2048], BF16, tag="wg", bufs=3, align_bytes=64, name="wg")
+            interleave(grp, raws.pop(s), pieces[s][1], mv)
+            grouped[s] = grp
+
+        def code_tiles(tag_c, tag_s, bufs):
+            cod = sb.tile([P, 512], U32, tag=tag_c, bufs=bufs, align_bytes=64, name=tag_c)
+            sca = sb.tile([P, 512], U8, tag=tag_s, bufs=bufs, align_bytes=64, name=tag_s)
+            return cod, sca
+
+        def quantize(grp, pair):
+            nc.vector.quantize_mx(out=pair[0][:].bitcast(FP8X4), scales=pair[1][:], in_=grp[:])
+
+        def quant(s):
+            if s < n_w + NB:
+                pair = code_tiles("wc", "ws", NB)
+            else:
+                xi = s - n_w - NB
+                pair = code_tiles("xc%d_%d" % (xi // 2, xi % 2), "xs%d_%d" % (xi // 2, xi % 2), 1)
+            quantize(grouped.pop(s), pair)
+            codes[s] = pair
+
+        def ticks(cap, mv):
+            n = 0
+            while n < cap and st["avail"] > 0 and st["q"] < n_pieces:
+                s = st["q"]
+                if s + 1 < n_pieces:
+                    copy(s + 1, mv)
+                quant(s)
+                if s + 1 + LD < n_pieces:
+                    load(s + 1 + LD)
+                st["q"] = s + 1
+                st["avail"] = st["avail"] - 1
+                n += 1
+
+        xraw = {}
+        xsrt = {}
+        xbank = {}
+        xgrp = {}
+        xcodes = {}
+
+        def xload(v):
+            h, n, gp = v // 16, (v % 16) // 8, v % 8
+            raw = sb.tile([P, 4, 1024], BF16, tag="big", bufs=3, name="xraw")
+            if v == 0:
+                for a in range(4):
+                    nc.sync.dma_start(out=raw[:, a, :], in_=x_units[h, n, :, a, 0:1024])
+            else:
+                nc.sync.dma_start(out=raw[:], in_=x_units[h, n, :, :, 1024 * gp : 1024 * (gp + 1)])
+            xraw[v] = raw
+
+        def xsort(v):
+            words = xraw.pop(v)[:].rearrange("p a k -> p (a k)").bitcast(F32)
+            for a in range(4):
+                srt = sb.tile([P, 512], F32, tag=SRT_TAGS[(4 * v + a) % 6], bufs=1, align_bytes=64, name="srt")
+                nc.vector.tensor_copy(
+                    out=srt[:].rearrange("p (g u q) -> p g u q", g=2, u=2),
+                    in_=words[:, 512 * a : 512 * (a + 1)].rearrange("p (g q u) -> p g u q", g=2, u=2),
+                )
+                xsrt[(v, a)] = srt
+            if v + 3 < 32:
+                xload(v + 3)
+
+        def transposes(v):
+            for gl in range(2):
+                for ap in range(2):
+                    bank = ps.tile([P, 512], F32, tag="b%d" % (4 + 2 * gl + ap), name="xt")
+                    for a2 in range(2):
+                        for u in range(2):
+                            base = 256 * gl + 128 * u
+                            col = 128 * (2 * a2 + u)
+                            nc.tensor.transpose(bank[:, col : col + 128], xsrt[(v, 2 * ap + a2)][:, base : base + 128], ident[:])
+                    xbank[(v, gl, ap)] = bank
+
+        def xevac(v):
+            for gl in range(2):
+                grp = sb.tile([P, 2048], BF16, tag="xg", bufs=4, align_bytes=64, name="xg")
+                gw = grp[:].bitcast(F32)
+                for ap in range(2):
+                    nc.scalar.copy(
+                        out=gw[:, 512 * ap : 512 * (ap + 1)].rearrange("p (a r u) -> p a r u", a=2, u=2),
+                        in_=xbank.pop((v, gl, ap))[:].rearrange("p (a u r) -> p a r u", a=2, u=2),
+                    )
+                xgrp[(v, gl)] = grp
+
+        def xquant(v):
+            n, gp = (v % 16) // 8, v % 8
+            for gl in range(2):
+                g = 2 * gp + gl
+                pair = code_tiles("xc%d_%d" % (g, n), "xs%d_%d" % (g, n), 1)
+                quantize(xgrp.pop((v, gl)), pair)
+                xcodes[(g, n)] = pair
+
+        def mx(bank, lhs, m0, rhs, start, stop):
+            nc.tensor.matmul_mx(
+                out=bank[:],
+                lhsT=lhs[0][:, m0 : m0 + P].bitcast(FP8X4),
+                lhsT_scale=lhs[1][:, m0 : m0 + P],
+                rhs=rhs[0][:].bitcast(FP8X4),
+                rhs_scale=rhs[1][:],
+                start=start,
+                stop=stop,
+            )
+
+        kvc = {}
+
+        def kv_evac(banks):
+            kvb = sb.tile([P, 4, 512], BF16, tag="xg", bufs=4, align_bytes=64, name="kvb")
+            for t in range(4):
+                if t % 2 == 0:
+                    nc.scalar.copy(out=kvb[:, t, :], in_=banks[t][:])
+                else:
+                    nc.vector.tensor_copy(out=kvb[:, t, :], in_=banks[t][:])
+            return kvb
+
+        def kv_copy(kvb):
+            grp = sb.tile([P, 2048], BF16, tag="wg", bufs=3, align_bytes=64, name="wg")
+            interleave(grp, kvb, False, 64)
+            return grp
+
+        def kv_quant(grp, c, hn):
+            pair = code_tiles("kc%d_%d" % (c, hn), "ks%d_%d" % (c, hn), 1)
+            quantize(grp, pair)
+            kvc[(c, hn)] = pair
+
+        pending = []
+
+        def kv_later(kvb, c, hn):
+            hold = {}
+
+            def job_copy():
+                hold["g"] = kv_copy(kvb)
+
+            def job_quant():
+                kv_quant(hold["g"], c, hn)
+
+            pending.append(job_copy)
+            pending.append(job_quant)
+
+        def run_pending():
+            if len(pending) > 0:
+                pending.pop(0)()
+
+        def acc_tiles(bank_ids):
+            out = []
+            for b in bank_ids:
+                acc = ps.tile([P, 512], F32, tag="b%d" % b, name="acc")
+                out.append(acc)
+            return out
+
+        xload(0)
+        load(0)
+        load(1)
+        xload(1)
+        load(2)
+        load(3)
+        xload(2)
+        xsort(0)
+        for h in range(2):
+            transposes(16 * h)
+            xsort(16 * h + 1)
+            xevac(16 * h)
+            if h == 0:
+                copy(0, 64)
+                ticks(2, 64)
+            xquant(16 * h)
+            acc = None
+            c0 = 3 * h
+            for u in range(16):
+                v = 16 * h + u
+                n, gp = u // 8, u % 8
+                if u + 1 < 16:
+                    transposes(v + 1)
+                    if u + 2 < 16:
+                        xsort(v + 2)
+                    xevac(v + 1)
+                if gp == 0:
+                    acc = acc_tiles((0, 1, 2, 3))
+                for gl in range(2):
+                    g = 2 * gp + gl
+                    for t in range(4):
+                        mx(acc[t], codes[w_piece[(h, c0, g)]], 128 * t, xcodes[(g, n)], g == 0, g == NG - 1)
+                if u + 1 < 16:
+                    xquant(v + 1)
+                if n == 1:
+                    codes.pop(w_piece[(h, c0, 2 * gp)])
+                    codes.pop(w_piece[(h, c0, 2 * gp + 1)])
+                    st["avail"] = st["avail"] + 2
+                if gp == 7:
+                    kv_later(kv_evac(acc), c0, 2 * h + n)
+                run_pending()
+                ticks(2 if n == 0 else gp % 2, 64)
+            if h == 0:
+                nc.sync.dma_start(out=fr[:], in_=freqs_cis.rearrange("(a p) f c -> p a (f c)", p=P))
+            for c in range(1 - h, 4 - h):
+                acc = acc_tiles(CELL_BANKS)
+                for g in range(NG):
+                    s = w_piece[(h, c, g)]
+                    for i in range(8):
+                        mx(acc[i], codes[s], 128 * (i % 4), xcodes[(g, 1 - i // 4)], g == 0, g == NG - 1)
+                    if h == 1 or c < 3:
+                        codes.pop(s)
+                        st["avail"] = st["avail"] + 1
+                    if g < NG - 1:
+                        run_pending()
+                        ticks(2 if g % 3 == 2 else 1, 64)
+                    if h == 0 and c == 3 and g == 8:
+                        xsort(16)
+                kv_later(kv_evac(acc[0:4]), c, 2 * h + 1)
+                kv_later(kv_evac(acc[4:8]), c, 2 * h)
+
+        st["avail"] = st["avail"] + 32
+        step = 0
+        for kind, grp_i in GROUPS:
+            width = 3 if kind == "k" else 2
+            dst_all = k_out if kind == "k" else v_out
+            for tt in range(16):
+                stg = sb.tile([P, 512 * width], F32, tag="big", bufs=3, name="stg")
+                for jj in range(width):
+                    bank = ps.tile([P, 512], F32, tag="b%d" % st["bank"], name="o")
+                    st["bank"] = (st["bank"] + 1) % 8
+                    for q in range(NQ):
+                        mx(bank, kvc[(q, tt // 4)], 128 * (tt % 4), codes[group_piece[(kind, grp_i, jj, q)]], q == 0, q == NQ - 1)
+                    if kind == "k" or jj == 0:
+                        nc.scalar.copy(out=stg[:, 512 * jj : 512 * (jj + 1)], in_=bank[:])
+                    else:
+                        nc.vector.tensor_copy(out=stg[:, 512 * jj : 512 * (jj + 1)], in_=bank[:])
+                if kind == "k":
+                    rot = stg[:].rearrange("p (h d) -> p h d", d=192)[:, :, 128:192].rearrange("p h (e f) -> p h e f", e=2)
+                    cs = fr[:, tt % 8, :].rearrange("p (f c) -> p c f", c=2)
+                    cosv = cs[:, 0:1, :].unsqueeze(1).to_broadcast([P, 8, 2, 32])
+                    sinv = cs[:, 1:2, :].unsqueeze(1).to_broadcast([P, 8, 2, 32])
+                    tmp = sb.tile([P, 8, 2, 32], F32, tag="xg", bufs=4, align_bytes=64, name="tmp")
+                    nc.vector.tensor_mul(out=tmp[:], in0=rot, in1=sinv)
+                    nc.vector.tensor_mul(out=rot, in0=rot, in1=cosv)
+                    nc.vector.tensor_sub(out=rot[:, :, 0, :], in0=rot[:, :, 0, :], in1=tmp[:, :, 1, :])
+                    nc.vector.tensor_add(out=rot[:, :, 1, :], in0=rot[:, :, 1, :], in1=tmp[:, :, 0, :])
+                col = 512 * width * grp_i
+                nc.sync.dma_start(out=dst_all[tt // 8, tt % 8, :, col : col + 512 * width], in_=stg[:])
+                run_pending()
+                if step % 2 == 0:
+                    ticks(1, 64)
+                step += 1

@@ -19,6 +19,7 @@ LD = 3
 GROUPS = (("k", 0), ("v", 0), ("k", 1), ("v", 1))
 CELL_BANKS = (4, 5, 6, 7, 0, 1, 2, 3)
 HALF_CHUNKS = ((0, 0), (0, 1), (0, 2), (0, 3), (1, 0), (1, 1), (1, 2))
+PART_TAGS = ("kc1_0", "kc1_1", "kc2_0", "kc2_1", "kc3_0", "kc3_1", "kc3_2", "kc3_3")
 SRT_TAGS = ("kc0_2", "kc0_3", "kc1_2", "kc1_3", "kc2_2", "kc2_3")
 
 
@@ -74,8 +75,9 @@ def tile_fa3mlaattention_pa_l_kernel(tc, x, freqs_cis, w_kv_down, w_k_up, w_v_up
             if permuted:
                 dst = grp[:].rearrange("p (t m j) -> p t m j", t=4, j=4)
                 src = raw[:].rearrange("p j (m t) -> p t m j", t=4)
-                nc.vector.tensor_copy(out=dst[:, :, 0:mv, :], in_=src[:, :, 0:mv, :])
-                nc.scalar.copy(out=dst[:, :, mv:P, :], in_=src[:, :, mv:P, :])
+                tv = mv // 32
+                nc.vector.tensor_copy(out=dst[:, 0:tv, :, :], in_=src[:, 0:tv, :, :])
+                nc.scalar.copy(out=dst[:, tv:4, :, :], in_=src[:, tv:4, :, :])
             else:
                 dst = grp[:].rearrange("p (c j) -> p c j", j=4)
                 src = raw[:].rearrange("p j c -> p c j")
@@ -123,8 +125,13 @@ def tile_fa3mlaattention_pa_l_kernel(tc, x, freqs_cis, w_kv_down, w_k_up, w_v_up
         xgrp = {}
         xcodes = {}
 
+        def unit(v):
+            h, u = v // 16, v % 16
+            per = 4 if h == 0 else 8
+            return h, (u % (2 * per)) // per, (u // (2 * per)) * per + u % per
+
         def xload(v):
-            h, n, gp = v // 16, (v % 16) // 8, v % 8
+            h, n, gp = unit(v)
             raw = sb.tile([P, 4, 1024], BF16, tag="big", bufs=3, name="xraw")
             if v == 0:
                 for a in range(4):
@@ -133,17 +140,21 @@ def tile_fa3mlaattention_pa_l_kernel(tc, x, freqs_cis, w_kv_down, w_k_up, w_v_up
                 nc.sync.dma_start(out=raw[:], in_=x_units[h, n, :, :, 1024 * gp : 1024 * (gp + 1)])
             xraw[v] = raw
 
-        def xsort(v):
-            words = xraw.pop(v)[:].rearrange("p a k -> p (a k)").bitcast(F32)
-            for a in range(4):
+        def xsort(v, a_lo, a_hi):
+            words = xraw[v][:].rearrange("p a k -> p (a k)").bitcast(F32)
+            for a in range(a_lo, a_hi):
                 srt = sb.tile([P, 512], F32, tag=SRT_TAGS[(4 * v + a) % 6], bufs=1, align_bytes=64, name="srt")
-                nc.vector.tensor_copy(
-                    out=srt[:].rearrange("p (g u q) -> p g u q", g=2, u=2),
-                    in_=words[:, 512 * a : 512 * (a + 1)].rearrange("p (g q u) -> p g u q", g=2, u=2),
-                )
+                dst = srt[:].rearrange("p (g u q) -> p g u q", g=2, u=2)
+                src = words[:, 512 * a : 512 * (a + 1)].rearrange("p (g q u) -> p g u q", g=2, u=2)
+                if a < 3:
+                    nc.vector.tensor_copy(out=dst, in_=src)
+                else:
+                    nc.scalar.copy(out=dst, in_=src)
                 xsrt[(v, a)] = srt
-            if v + 3 < 32:
-                xload(v + 3)
+            if a_hi == 4:
+                xraw.pop(v)
+                if v + 3 < 32:
+                    xload(v + 3)
 
         def transposes(v):
             for gl in range(2):
@@ -168,7 +179,7 @@ def tile_fa3mlaattention_pa_l_kernel(tc, x, freqs_cis, w_kv_down, w_k_up, w_v_up
                 xgrp[(v, gl)] = grp
 
         def xquant(v):
-            n, gp = (v % 16) // 8, v % 8
+            h, n, gp = unit(v)
             for gl in range(2):
                 g = 2 * gp + gl
                 pair = code_tiles("xc%d_%d" % (g, n), "xs%d_%d" % (g, n), 1)
@@ -187,6 +198,7 @@ def tile_fa3mlaattention_pa_l_kernel(tc, x, freqs_cis, w_kv_down, w_k_up, w_v_up
             )
 
         kvc = {}
+        parts = {}
 
         def kv_evac(banks):
             kvb = sb.tile([P, 4, 512], BF16, tag="xg", bufs=4, align_bytes=64, name="kvb")
@@ -195,6 +207,21 @@ def tile_fa3mlaattention_pa_l_kernel(tc, x, freqs_cis, w_kv_down, w_k_up, w_v_up
                     nc.scalar.copy(out=kvb[:, t, :], in_=banks[t][:])
                 else:
                     nc.vector.tensor_copy(out=kvb[:, t, :], in_=banks[t][:])
+            return kvb
+
+        def part_evac(banks, n):
+            for t in range(4):
+                par = sb.tile([P, 512], F32, tag=PART_TAGS[4 * n + t], bufs=1, align_bytes=64, name="par")
+                if t % 2 == 0:
+                    nc.scalar.copy(out=par[:], in_=banks[t][:])
+                else:
+                    nc.vector.tensor_copy(out=par[:], in_=banks[t][:])
+                parts[(n, t)] = par
+
+        def kv_evac_add(banks, n):
+            kvb = sb.tile([P, 4, 512], BF16, tag="xg", bufs=4, align_bytes=64, name="kvb")
+            for t in range(4):
+                nc.vector.tensor_add(out=kvb[:, t, :], in0=banks[t][:], in1=parts.pop((n, t))[:])
             return kvb
 
         def kv_copy(kvb):
@@ -239,11 +266,12 @@ def tile_fa3mlaattention_pa_l_kernel(tc, x, freqs_cis, w_kv_down, w_k_up, w_v_up
         load(2)
         load(3)
         xload(2)
-        xsort(0)
+        xsort(0, 0, 4)
         for h in range(2):
             transposes(16 * h)
-            xsort(16 * h + 1)
+            xsort(16 * h + 1, 0, 3)
             xevac(16 * h)
+            xsort(16 * h + 1, 3, 4)
             if h == 0:
                 copy(0, 64)
                 ticks(2, 64)
@@ -252,28 +280,36 @@ def tile_fa3mlaattention_pa_l_kernel(tc, x, freqs_cis, w_kv_down, w_k_up, w_v_up
             c0 = 3 * h
             for u in range(16):
                 v = 16 * h + u
-                n, gp = u // 8, u % 8
+                n, gp = unit(v)[1], unit(v)[2]
+                per = 4 if h == 0 else 8
                 if u + 1 < 16:
                     transposes(v + 1)
                     if u + 2 < 16:
-                        xsort(v + 2)
+                        xsort(v + 2, 0, 3)
                     xevac(v + 1)
-                if gp == 0:
+                    if u + 2 < 16:
+                        xsort(v + 2, 3, 4)
+                if gp % per == 0:
                     acc = acc_tiles((0, 1, 2, 3))
                 for gl in range(2):
                     g = 2 * gp + gl
                     for t in range(4):
-                        mx(acc[t], codes[w_piece[(h, c0, g)]], 128 * t, xcodes[(g, n)], g == 0, g == NG - 1)
+                        mx(acc[t], codes[w_piece[(h, c0, g)]], 128 * t, xcodes[(g, n)], g % (2 * per) == 0, g % (2 * per) == 2 * per - 1)
                 if u + 1 < 16:
                     xquant(v + 1)
                 if n == 1:
                     codes.pop(w_piece[(h, c0, 2 * gp)])
                     codes.pop(w_piece[(h, c0, 2 * gp + 1)])
                     st["avail"] = st["avail"] + 2
-                if gp == 7:
-                    kv_later(kv_evac(acc), c0, 2 * h + n)
+                if gp % per == per - 1:
+                    if h == 1:
+                        kv_later(kv_evac(acc), c0, 2 * h + n)
+                    elif gp < 4:
+                        part_evac(acc, n)
+                    else:
+                        kv_later(kv_evac_add(acc, n), c0, 2 * h + n)
                 run_pending()
-                ticks(2 if n == 0 else gp % 2, 64)
+                ticks(2 if v < 4 else ((1 if u % 4 != 3 else 0) if h == 0 else u % 2), 64)
             if h == 0:
                 nc.sync.dma_start(out=fr[:], in_=freqs_cis.rearrange("(a p) f c -> p a (f c)", p=P))
             for c in range(1 - h, 4 - h):
@@ -289,7 +325,7 @@ def tile_fa3mlaattention_pa_l_kernel(tc, x, freqs_cis, w_kv_down, w_k_up, w_v_up
                         run_pending()
                         ticks(2 if g % 3 == 2 else 1, 64)
                     if h == 0 and c == 3 and g == 8:
-                        xsort(16)
+                        xsort(16, 0, 4)
                 kv_later(kv_evac(acc[0:4]), c, 2 * h + 1)
                 kv_later(kv_evac(acc[4:8]), c, 2 * h)
 

@@ -15,11 +15,10 @@ P = 128
 NG = 16
 NQ = 4
 NB = 17
-LD = 3
+LD = 4
 GROUPS = (("k", 0), ("v", 0), ("k", 1), ("v", 1))
 CELL_BANKS = (4, 5, 6, 7, 0, 1, 2, 3)
 HALF_CHUNKS = ((0, 0), (0, 1), (0, 2), (0, 3), (1, 0), (1, 1), (1, 2))
-PART_TAGS = ("kc1_0", "kc1_1", "kc2_0", "kc2_1", "kc3_0", "kc3_1", "kc3_2", "kc3_3")
 SRT_TAGS = ("kc0_2", "kc0_3", "kc1_2", "kc1_3", "kc2_2", "kc2_3")
 
 
@@ -125,13 +124,8 @@ def tile_fa3mlaattention_pa_l_kernel(tc, x, freqs_cis, w_kv_down, w_k_up, w_v_up
         xgrp = {}
         xcodes = {}
 
-        def unit(v):
-            h, u = v // 16, v % 16
-            per = 4 if h == 0 else 8
-            return h, (u % (2 * per)) // per, (u // (2 * per)) * per + u % per
-
         def xload(v):
-            h, n, gp = unit(v)
+            h, n, gp = v // 16, (v % 16) // 8, v % 8
             raw = sb.tile([P, 4, 1024], BF16, tag="big", bufs=3, name="xraw")
             if v == 0:
                 for a in range(4):
@@ -140,21 +134,17 @@ def tile_fa3mlaattention_pa_l_kernel(tc, x, freqs_cis, w_kv_down, w_k_up, w_v_up
                 nc.sync.dma_start(out=raw[:], in_=x_units[h, n, :, :, 1024 * gp : 1024 * (gp + 1)])
             xraw[v] = raw
 
-        def xsort(v, a_lo, a_hi):
-            words = xraw[v][:].rearrange("p a k -> p (a k)").bitcast(F32)
-            for a in range(a_lo, a_hi):
+        def xsort(v):
+            words = xraw.pop(v)[:].rearrange("p a k -> p (a k)").bitcast(F32)
+            for a in range(4):
                 srt = sb.tile([P, 512], F32, tag=SRT_TAGS[(4 * v + a) % 6], bufs=1, align_bytes=64, name="srt")
-                dst = srt[:].rearrange("p (g u q) -> p g u q", g=2, u=2)
-                src = words[:, 512 * a : 512 * (a + 1)].rearrange("p (g q u) -> p g u q", g=2, u=2)
-                if a < 3:
-                    nc.vector.tensor_copy(out=dst, in_=src)
-                else:
-                    nc.scalar.copy(out=dst, in_=src)
+                nc.vector.tensor_copy(
+                    out=srt[:].rearrange("p (g u q) -> p g u q", g=2, u=2),
+                    in_=words[:, 512 * a : 512 * (a + 1)].rearrange("p (g q u) -> p g u q", g=2, u=2),
+                )
                 xsrt[(v, a)] = srt
-            if a_hi == 4:
-                xraw.pop(v)
-                if v + 3 < 32:
-                    xload(v + 3)
+            if v + 3 < 32:
+                xload(v + 3)
 
         def transposes(v):
             for gl in range(2):
@@ -179,7 +169,7 @@ def tile_fa3mlaattention_pa_l_kernel(tc, x, freqs_cis, w_kv_down, w_k_up, w_v_up
                 xgrp[(v, gl)] = grp
 
         def xquant(v):
-            h, n, gp = unit(v)
+            n, gp = (v % 16) // 8, v % 8
             for gl in range(2):
                 g = 2 * gp + gl
                 pair = code_tiles("xc%d_%d" % (g, n), "xs%d_%d" % (g, n), 1)
@@ -198,7 +188,6 @@ def tile_fa3mlaattention_pa_l_kernel(tc, x, freqs_cis, w_kv_down, w_k_up, w_v_up
             )
 
         kvc = {}
-        parts = {}
 
         def kv_evac(banks):
             kvb = sb.tile([P, 4, 512], BF16, tag="xg", bufs=4, align_bytes=64, name="kvb")
@@ -207,21 +196,6 @@ def tile_fa3mlaattention_pa_l_kernel(tc, x, freqs_cis, w_kv_down, w_k_up, w_v_up
                     nc.scalar.copy(out=kvb[:, t, :], in_=banks[t][:])
                 else:
                     nc.vector.tensor_copy(out=kvb[:, t, :], in_=banks[t][:])
-            return kvb
-
-        def part_evac(banks, n):
-            for t in range(4):
-                par = sb.tile([P, 512], F32, tag=PART_TAGS[4 * n + t], bufs=1, align_bytes=64, name="par")
-                if t % 2 == 0:
-                    nc.scalar.copy(out=par[:], in_=banks[t][:])
-                else:
-                    nc.vector.tensor_copy(out=par[:], in_=banks[t][:])
-                parts[(n, t)] = par
-
-        def kv_evac_add(banks, n):
-            kvb = sb.tile([P, 4, 512], BF16, tag="xg", bufs=4, align_bytes=64, name="kvb")
-            for t in range(4):
-                nc.vector.tensor_add(out=kvb[:, t, :], in0=banks[t][:], in1=parts.pop((n, t))[:])
             return kvb
 
         def kv_copy(kvb):
@@ -266,12 +240,12 @@ def tile_fa3mlaattention_pa_l_kernel(tc, x, freqs_cis, w_kv_down, w_k_up, w_v_up
         load(2)
         load(3)
         xload(2)
-        xsort(0, 0, 4)
+        load(4)
+        xsort(0)
         for h in range(2):
             transposes(16 * h)
-            xsort(16 * h + 1, 0, 3)
+            xsort(16 * h + 1)
             xevac(16 * h)
-            xsort(16 * h + 1, 3, 4)
             if h == 0:
                 copy(0, 64)
                 ticks(2, 64)
@@ -280,36 +254,28 @@ def tile_fa3mlaattention_pa_l_kernel(tc, x, freqs_cis, w_kv_down, w_k_up, w_v_up
             c0 = 3 * h
             for u in range(16):
                 v = 16 * h + u
-                n, gp = unit(v)[1], unit(v)[2]
-                per = 4 if h == 0 else 8
+                n, gp = u // 8, u % 8
                 if u + 1 < 16:
                     transposes(v + 1)
                     if u + 2 < 16:
-                        xsort(v + 2, 0, 3)
+                        xsort(v + 2)
                     xevac(v + 1)
-                    if u + 2 < 16:
-                        xsort(v + 2, 3, 4)
-                if gp % per == 0:
+                if gp == 0:
                     acc = acc_tiles((0, 1, 2, 3))
                 for gl in range(2):
                     g = 2 * gp + gl
                     for t in range(4):
-                        mx(acc[t], codes[w_piece[(h, c0, g)]], 128 * t, xcodes[(g, n)], g % (2 * per) == 0, g % (2 * per) == 2 * per - 1)
+                        mx(acc[t], codes[w_piece[(h, c0, g)]], 128 * t, xcodes[(g, n)], g == 0, g == NG - 1)
                 if u + 1 < 16:
                     xquant(v + 1)
                 if n == 1:
                     codes.pop(w_piece[(h, c0, 2 * gp)])
                     codes.pop(w_piece[(h, c0, 2 * gp + 1)])
                     st["avail"] = st["avail"] + 2
-                if gp % per == per - 1:
-                    if h == 1:
-                        kv_later(kv_evac(acc), c0, 2 * h + n)
-                    elif gp < 4:
-                        part_evac(acc, n)
-                    else:
-                        kv_later(kv_evac_add(acc, n), c0, 2 * h + n)
+                if gp == 7:
+                    kv_later(kv_evac(acc), c0, 2 * h + n)
                 run_pending()
-                ticks(2 if v < 4 else ((1 if u % 4 != 3 else 0) if h == 0 else u % 2), 64)
+                ticks(2 if n == 0 else gp % 2, 64)
             if h == 0:
                 nc.sync.dma_start(out=fr[:], in_=freqs_cis.rearrange("(a p) f c -> p a (f c)", p=P))
             for c in range(1 - h, 4 - h):
@@ -325,7 +291,7 @@ def tile_fa3mlaattention_pa_l_kernel(tc, x, freqs_cis, w_kv_down, w_k_up, w_v_up
                         run_pending()
                         ticks(2 if g % 3 == 2 else 1, 64)
                     if h == 0 and c == 3 and g == 8:
-                        xsort(16, 0, 4)
+                        xsort(16)
                 kv_later(kv_evac(acc[0:4]), c, 2 * h + 1)
                 kv_later(kv_evac(acc[4:8]), c, 2 * h)
 

@@ -189,13 +189,16 @@ def tile_fa3mlaattention_pa_l_kernel(tc, x, freqs_cis, w_kv_down, w_k_up, w_v_up
 
         kvc = {}
 
+        def kv_bank(kvb, t, bank):
+            if t % 2 == 0:
+                nc.scalar.copy(out=kvb[:, t, :], in_=bank[:])
+            else:
+                nc.vector.tensor_copy(out=kvb[:, t, :], in_=bank[:])
+
         def kv_evac(banks):
             kvb = sb.tile([P, 4, 512], BF16, tag="xg", bufs=4, align_bytes=64, name="kvb")
             for t in range(4):
-                if t % 2 == 0:
-                    nc.scalar.copy(out=kvb[:, t, :], in_=banks[t][:])
-                else:
-                    nc.vector.tensor_copy(out=kvb[:, t, :], in_=banks[t][:])
+                kv_bank(kvb, t, banks[t])
             return kvb
 
         def kv_copy(kvb):
@@ -262,9 +265,8 @@ def tile_fa3mlaattention_pa_l_kernel(tc, x, freqs_cis, w_kv_down, w_k_up, w_v_up
                     xevac(v + 1)
                 if gp == 0:
                     acc = acc_tiles((0, 1, 2, 3))
-                for gl in range(2):
-                    g = 2 * gp + gl
-                    for t in range(4):
+                for t in range(4):
+                    for g in (2 * gp, 2 * gp + 1):
                         mx(acc[t], codes[w_piece[(h, c0, g)]], 128 * t, xcodes[(g, n)], g == 0, g == NG - 1)
                 if u + 1 < 16:
                     xquant(v + 1)
@@ -280,20 +282,26 @@ def tile_fa3mlaattention_pa_l_kernel(tc, x, freqs_cis, w_kv_down, w_k_up, w_v_up
                 nc.sync.dma_start(out=fr[:], in_=freqs_cis.rearrange("(a p) f c -> p a (f c)", p=P))
             for c in range(1 - h, 4 - h):
                 acc = acc_tiles(CELL_BANKS)
-                for g in range(NG):
-                    s = w_piece[(h, c, g)]
+                for gq in range(4):
+                    kvb = None
                     for i in range(8):
-                        mx(acc[i], codes[s], 128 * (i % 4), xcodes[(g, 1 - i // 4)], g == 0, g == NG - 1)
+                        for g in range(4 * gq, 4 * gq + 4):
+                            mx(acc[i], codes[w_piece[(h, c, g)]], 128 * (i % 4), xcodes[(g, 1 - i // 4)], g == 0, g == NG - 1)
+                        if gq == 3:
+                            if i % 4 == 0:
+                                kvb = sb.tile([P, 4, 512], BF16, tag="xg", bufs=4, align_bytes=64, name="kvb")
+                            kv_bank(kvb, i % 4, acc[i])
+                            if i % 4 == 3:
+                                kv_later(kvb, c, 2 * h + 1 - i // 4)
                     if h == 1 or c < 3:
-                        codes.pop(s)
-                        st["avail"] = st["avail"] + 1
-                    if g < NG - 1:
-                        run_pending()
-                        ticks(2 if g % 3 == 2 else 1, 64)
-                    if h == 0 and c == 3 and g == 8:
+                        for g in range(4 * gq, 4 * gq + 4):
+                            codes.pop(w_piece[(h, c, g)])
+                        st["avail"] = st["avail"] + 4
+                    run_pending()
+                    ticks(5, 64)
+                    run_pending()
+                    if h == 0 and c == 3 and gq == 2:
                         xsort(16)
-                kv_later(kv_evac(acc[0:4]), c, 2 * h + 1)
-                kv_later(kv_evac(acc[4:8]), c, 2 * h)
 
         st["avail"] = st["avail"] + 32
         step = 0

from contextlib import ExitStack

import concourse.mybir as mybir
from concourse.masks import make_identity

FLOPS = 2 * 2048 * 8192 * 2048 + 2 * 2048 * 2048 * 5120

F32 = mybir.dt.float32
BF16 = mybir.dt.bfloat16
U32 = mybir.dt.uint32
U8 = mybir.dt.uint8
FP8X4 = mybir.dt.float8_e4m3fn_x4

P = 128
NG = 16
NQ = 4
NB = 17
LD = 4
GROUPS = (("k", 0), ("v", 0), ("k", 1), ("v", 1))
CELL_BANKS = (4, 5, 6, 7, 0, 1, 2, 3)
HALF_CHUNKS = ((0, 0), (0, 1), (0, 2), (0, 3), (1, 0), (1, 1), (1, 2))
SRT_TAGS = ("kc0_2", "kc0_3", "kc1_2", "kc1_3", "kc2_2", "kc2_3")


def tile_fa3mlaattention_pa_l_kernel(tc, x, freqs_cis, w_kv_down, w_k_up, w_v_up, out_0, out_1):
    nc = tc.nc
    with ExitStack() as ctx:
        sb = ctx.enter_context(tc.tile_pool(name="sb", bufs=1))
        ps = ctx.enter_context(tc.psum_pool(name="ps", bufs=1))
        ctx.enter_context(tc.manual_schedule())

        x_units = x.rearrange("b (n a p) k -> b n p a k", a=4, p=P)
        wd = w_kv_down.rearrange("(g p j) c -> g p j c", p=P, j=4)
        wk = w_k_up.rearrange("(q p j) c -> q p j c", p=P, j=4)
        wv = w_v_up.rearrange("(q p j) c -> q p j c", p=P, j=4)
        k_out = out_0.rearrange("b (a p) h d -> b a p (h d)", p=P)
        v_out = out_1.rearrange("b (a p) h d -> b a p (h d)", p=P)

        ident = sb.tile([P, P], F32, name="ident")
        make_identity(nc, ident[:])
        fr = sb.tile([P, 8, 64], BF16, name="fr")

        pieces = []
        w_piece = {}
        for h, c in HALF_CHUNKS:
            for g in range(NG):
                w_piece[(h, c, g)] = len(pieces)
                pieces.append((wd[g, :, :, 512 * c : 512 * (c + 1)], True))
        for g in range(NG):
            w_piece[(1, 3, g)] = w_piece[(0, 3, g)]
        group_piece = {}
        for kind, grp_i in GROUPS:
            width = 3 if kind == "k" else 2
            src = wk if kind == "k" else wv
            for jj in range(width):
                col = 512 * (width * grp_i + jj)
                for q in range(NQ):
                    group_piece[(kind, grp_i, jj, q)] = len(pieces)
                    pieces.append((src[q, :, :, col : col + 512], False))
        n_pieces = len(pieces)
        n_w = len(HALF_CHUNKS) * NG

        raws = {}
        grouped = {}
        codes = {}
        st = {"q": 0, "avail": NB, "bank": 4}

        def load(s):
            raw = sb.tile([P, 4, 512], BF16, tag="raw", bufs=LD + 1, name="raw")
            nc.sync.dma_start(out=raw[:], in_=pieces[s][0])
            raws[s] = raw

        def interleave(grp, raw, permuted, mv):
            if permuted:
                dst = grp[:].rearrange("p (t m j) -> p t m j", t=4, j=4)
                src = raw[:].rearrange("p j (m t) -> p t m j", t=4)
                tv = mv // 32
                nc.vector.tensor_copy(out=dst[:, 0:tv, :, :], in_=src[:, 0:tv, :, :])
                nc.scalar.copy(out=dst[:, tv:4, :, :], in_=src[:, tv:4, :, :])
            else:
                dst = grp[:].rearrange("p (c j) -> p c j", j=4)
                src = raw[:].rearrange("p j c -> p c j")
                nc.vector.tensor_copy(out=dst[:, 0 : 4 * mv, :], in_=src[:, 0 : 4 * mv, :])
                nc.scalar.copy(out=dst[:, 4 * mv : 512, :], in_=src[:, 4 * mv : 512, :])

        def copy(s, mv):
            grp = sb.tile([P, 2048], BF16, tag="wg", bufs=3, align_bytes=64, name="wg")
            interleave(grp, raws.pop(s), pieces[s][1], mv)
            grouped[s] = grp

        def code_tiles(tag_c, tag_s, bufs):
            cod = sb.tile([P, 512], U32, tag=tag_c, bufs=bufs, align_bytes=64, name=tag_c)
            sca = sb.tile([P, 512], U8, tag=tag_s, bufs=bufs, align_bytes=64, name=tag_s)
            return cod, sca

        def quantize(grp, pair):
            nc.vector.quantize_mx(out=pair[0][:].bitcast(FP8X4), scales=pair[1][:], in_=grp[:])

        def quant(s):
            if s < n_w + NB:
                pair = code_tiles("wc", "ws", NB)
            else:
                xi = s - n_w - NB
                pair = code_tiles("xc%d_%d" % (xi // 2, xi % 2), "xs%d_%d" % (xi // 2, xi % 2), 1)
            quantize(grouped.pop(s), pair)
            codes[s] = pair

        def ticks(cap, mv):
            n = 0
            while n < cap and st["avail"] > 0 and st["q"] < n_pieces:
                s = st["q"]
                if s + 1 < n_pieces:
                    copy(s + 1, mv)
                quant(s)
                if s + 1 + LD < n_pieces:
                    load(s + 1 + LD)
                st["q"] = s + 1
                st["avail"] = st["avail"] - 1
                n += 1

        xraw = {}
        xsrt = {}
        xbank = {}
        xgrp = {}
        xcodes = {}

        def xload(v):
            h, n, gp = v // 16, (v % 16) // 8, v % 8
            raw = sb.tile([P, 4, 1024], BF16, tag="big", bufs=3, name="xraw")
            if v == 0:
                for a in range(4):
                    nc.sync.dma_start(out=raw[:, a, :], in_=x_units[h, n, :, a, 0:1024])
            else:
                nc.sync.dma_start(out=raw[:], in_=x_units[h, n, :, :, 1024 * gp : 1024 * (gp + 1)])
            xraw[v] = raw

        def xsort(v):
            words = xraw.pop(v)[:].rearrange("p a k -> p (a k)").bitcast(F32)
            for a in range(4):
                srt = sb.tile([P, 512], F32, tag=SRT_TAGS[(4 * v + a) % 6], bufs=1, align_bytes=64, name="srt")
                nc.vector.tensor_copy(
                    out=srt[:].rearrange("p (g u q) -> p g u q", g=2, u=2),
                    in_=words[:, 512 * a : 512 * (a + 1)].rearrange("p (g q u) -> p g u q", g=2, u=2),
                )
                xsrt[(v, a)] = srt
            if v + 3 < 32:
                xload(v + 3)

        def transposes(v):
            for gl in range(2):
                for ap in range(2):
                    bank = ps.tile([P, 512], F32, tag="b%d" % (4 + 2 * gl + ap), name="xt")
                    for a2 in range(2):
                        for u in range(2):
                            base = 256 * gl + 128 * u
                            col = 128 * (2 * a2 + u)
                            nc.tensor.transpose(bank[:, col : col + 128], xsrt[(v, 2 * ap + a2)][:, base : base + 128], ident[:])
                    xbank[(v, gl, ap)] = bank

        def xevac(v):
            for gl in range(2):
                grp = sb.tile([P, 2048], BF16, tag="xg", bufs=4, align_bytes=64, name="xg")
                gw = grp[:].bitcast(F32)
                for ap in range(2):
                    nc.scalar.copy(
                        out=gw[:, 512 * ap : 512 * (ap + 1)].rearrange("p (a r u) -> p a r u", a=2, u=2),
                        in_=xbank.pop((v, gl, ap))[:].rearrange("p (a u r) -> p a r u", a=2, u=2),
                    )
                xgrp[(v, gl)] = grp

        def xquant(v):
            n, gp = (v % 16) // 8, v % 8
            for gl in range(2):
                g = 2 * gp + gl
                pair = code_tiles("xc%d_%d" % (g, n), "xs%d_%d" % (g, n), 1)
                quantize(xgrp.pop((v, gl)), pair)
                xcodes[(g, n)] = pair

        def mx(bank, lhs, m0, rhs, start, stop):
            nc.tensor.matmul_mx(
                out=bank[:],
                lhsT=lhs[0][:, m0 : m0 + P].bitcast(FP8X4),
                lhsT_scale=lhs[1][:, m0 : m0 + P],
                rhs=rhs[0][:].bitcast(FP8X4),
                rhs_scale=rhs[1][:],
                start=start,
                stop=stop,
            )

        kvc = {}

        def kv_bank(kvb, t, bank):
            if t % 2 == 0:
                nc.scalar.copy(out=kvb[:, t, :], in_=bank[:])
            else:
                nc.vector.tensor_copy(out=kvb[:, t, :], in_=bank[:])

        def kv_evac(banks):
            kvb = sb.tile([P, 4, 512], BF16, tag="xg", bufs=4, align_bytes=64, name="kvb")
            for t in range(4):
                kv_bank(kvb, t, banks[t])
            return kvb

        def kv_copy(kvb):
            grp = sb.tile([P, 2048], BF16, tag="wg", bufs=3, align_bytes=64, name="wg")
            interleave(grp, kvb, False, 64)
            return grp

        def kv_quant(grp, c, hn):
            pair = code_tiles("kc%d_%d" % (c, hn), "ks%d_%d" % (c, hn), 1)
            quantize(grp, pair)
            kvc[(c, hn)] = pair

        pending = []

        def kv_later(kvb, c, hn):
            hold = {}

            def job_copy():
                hold["g"] = kv_copy(kvb)

            def job_quant():
                kv_quant(hold["g"], c, hn)

            pending.append(job_copy)
            pending.append(job_quant)

        def run_pending():
            if len(pending) > 0:
                pending.pop(0)()

        def acc_tiles(bank_ids):
            out = []
            for b in bank_ids:
                acc = ps.tile([P, 512], F32, tag="b%d" % b, name="acc")
                out.append(acc)
            return out

        xload(0)
        load(0)
        load(1)
        xload(1)
        load(2)
        load(3)
        xload(2)
        load(4)
        xsort(0)
        for h in range(2):
            transposes(16 * h)
            xsort(16 * h + 1)
            xevac(16 * h)
            if h == 0:
                copy(0, 64)
                ticks(2, 64)
            xquant(16 * h)
            acc = None
            c0 = 3 * h
            for u in range(16):
                v = 16 * h + u
                n, gp = u // 8, u % 8
                if u + 1 < 16:
                    transposes(v + 1)
                    if u + 2 < 16:
                        xsort(v + 2)
                    xevac(v + 1)
                if gp == 0:
                    acc = acc_tiles((0, 1, 2, 3))
                for t in range(4):
                    for g in (2 * gp, 2 * gp + 1):
                        mx(acc[t], codes[w_piece[(h, c0, g)]], 128 * t, xcodes[(g, n)], g == 0, g == NG - 1)
                if u + 1 < 16:
                    xquant(v + 1)
                if n == 1:
                    codes.pop(w_piece[(h, c0, 2 * gp)])
                    codes.pop(w_piece[(h, c0, 2 * gp + 1)])
                    st["avail"] = st["avail"] + 2
                if gp == 7:
                    kv_later(kv_evac(acc), c0, 2 * h + n)
                run_pending()
                ticks(2 if n == 0 else gp % 2, 64)
            if h == 0:
                nc.sync.dma_start(out=fr[:], in_=freqs_cis.rearrange("(a p) f c -> p a (f c)", p=P))
            for c in range(1 - h, 4 - h):
                acc = acc_tiles(CELL_BANKS)
                for gq in range(4):
                    kvb = None
                    for i in range(8):
                        for g in range(4 * gq, 4 * gq + 4):
                            mx(acc[i], codes[w_piece[(h, c, g)]], 128 * (i % 4), xcodes[(g, 1 - i // 4)], g == 0, g == NG - 1)
                        if gq == 3:
                            if i % 4 == 0:
                                kvb = sb.tile([P, 4, 512], BF16, tag="xg", bufs=4, align_bytes=64, name="kvb")
                            kv_bank(kvb, i % 4, acc[i])
                            if i % 4 == 3:
                                kv_later(kvb, c, 2 * h + 1 - i // 4)
                    if h == 1 or c < 3:
                        for g in range(4 * gq, 4 * gq + 4):
                            codes.pop(w_piece[(h, c, g)])
                        st["avail"] = st["avail"] + 4
                    run_pending()
                    ticks(5, 64)
                    run_pending()
                    if h == 0 and c == 3 and gq == 2:
                        xsort(16)

        st["avail"] = st["avail"] + 32
        step = 0
        for kind, grp_i in GROUPS:
            width = 3 if kind == "k" else 2
            dst_all = k_out if kind == "k" else v_out
            for tt in range(16):
                stg = sb.tile([P, 512 * width], F32, tag="big", bufs=3, name="stg")
                for jj in range(width):
                    bank = ps.tile([P, 512], F32, tag="b%d" % st["bank"], name="o")
                    st["bank"] = (st["bank"] + 1) % 8
                    for q in range(NQ):
                        mx(bank, kvc[(q, tt // 4)], 128 * (tt % 4), codes[group_piece[(kind, grp_i, jj, q)]], q == 0, q == NQ - 1)
                    if kind == "k" or jj == 0:
                        nc.scalar.copy(out=stg[:, 512 * jj : 512 * (jj + 1)], in_=bank[:])
                    else:
                        nc.vector.tensor_copy(out=stg[:, 512 * jj : 512 * (jj + 1)], in_=bank[:])
                if kind == "k":
                    rot = stg[:].rearrange("p (h d) -> p h d", d=192)[:, :, 128:192].rearrange("p h (e f) -> p h e f", e=2)
                    cs = fr[:, tt % 8, :].rearrange("p (f c) -> p c f", c=2)
                    cosv = cs[:, 0:1, :].unsqueeze(1).to_broadcast([P, 8, 2, 32])
                    sinv = cs[:, 1:2, :].unsqueeze(1).to_broadcast([P, 8, 2, 32])
                    tmp = sb.tile([P, 8, 2, 32], F32, tag="xg", bufs=4, align_bytes=64, name="tmp")
                    nc.vector.tensor_mul(out=tmp[:], in0=rot, in1=sinv)
                    nc.vector.tensor_mul(out=rot, in0=rot, in1=cosv)
                    nc.vector.tensor_sub(out=rot[:, :, 0, :], in0=rot[:, :, 0, :], in1=tmp[:, :, 1, :])
                    nc.vector.tensor_add(out=rot[:, :, 1, :], in0=rot[:, :, 1, :], in1=tmp[:, :, 0, :])
                col = 512 * width * grp_i
                nc.sync.dma_start(out=dst_all[tt // 8, tt % 8, :, col : col + 512 * width], in_=stg[:])
                run_pending()
                if step % 2 == 0:
                    ticks(1, 64)
                step += 1
